import numpy as np
import ml_dtypes


def mxq(x, axis, fmt="e4m3"):
    dtype, down = {"e4m3": (ml_dtypes.float8_e4m3fn, 7), "e5m2": (ml_dtypes.float8_e5m2, 14)}[fmt]
    v = np.moveaxis(np.asarray(x, np.float32).astype(ml_dtypes.bfloat16).astype(np.float64), axis, -1)
    blocks = v.reshape(v.shape[:-1] + (-1, 32))
    amax = np.abs(blocks).max(-1, keepdims=True)
    byte = np.maximum(np.where(amax > 0, np.frexp(amax)[1] - 1 + 127, 0) - down, 1)
    scale = np.exp2(byte - 127.0)
    codes = (blocks / scale).astype(np.float32).astype(dtype).astype(np.float64)
    return np.moveaxis((codes * scale).reshape(v.shape), -1, axis)


WIDE = False


def mx_kscale(k):
    if not WIDE:
        return np.ones(k)
    levels = np.array([10, -10, 5, -5, 0])
    a = np.random.permutation(np.resize(levels, k // 512 * 4)).reshape(k // 512, 4)
    idx = np.arange(k)
    return np.exp2(a[idx // 512, idx % 128 // 32])


BF16 = ml_dtypes.bfloat16


def bf(x):
    return np.asarray(x, np.float32).astype(BF16)


def f64(x):
    return np.asarray(x).astype(np.float64)


E2M1 = np.array([0.0, 0.5, 1.0, 1.5, 2.0, 3.0, 4.0, 6.0, -0.0, -0.5, -1.0, -1.5, -2.0, -3.0, -4.0, -6.0])


def pack_weight(w, fmt):
    k, n = w.shape
    w = f64(bf(w)).reshape(k // 32, 32, n)
    amax = np.abs(w).max(1)
    if fmt == "e4m3":
        byte = np.frexp(amax)[1] - 1 + 127 - 7
    else:
        mant, ex = np.frexp(amax / 6.0)
        byte = np.where(mant > 0.5, ex, ex - 1) + 127
    byte = np.clip(np.where(amax > 0, byte, 1), 1, 254)
    scaled = (w * np.exp2(127.0 - byte)[:, None, :]).reshape(k, n).astype(np.float32)
    by_word = np.ascontiguousarray(scaled.reshape(k // 512, 128, 4, n).transpose(0, 1, 3, 2))
    if fmt == "e4m3":
        words = by_word.astype(ml_dtypes.float8_e4m3fn).view(np.uint8)
    else:
        c = by_word.astype(ml_dtypes.float4_e2m1fn).view(np.uint8) & 0xF
        words = c[..., 0::2] | (c[..., 1::2] << 4)
    return np.ascontiguousarray(words), np.ascontiguousarray(byte.astype(np.uint8).reshape(k // 512, 16, n))


def unpack_weight(words, scales, fmt):
    g, p, n, _ = words.shape
    if fmt == "e4m3":
        vals = np.ascontiguousarray(words).view(ml_dtypes.float8_e4m3fn).astype(np.float64)
    else:
        nib = np.empty((g, p, n, 4), np.uint8)
        nib[..., 0::2] = words & 0xF
        nib[..., 1::2] = words >> 4
        vals = E2M1[nib]
    vals = vals * np.repeat(np.exp2(scales.astype(np.float64) - 127.0), 8, axis=1)[..., None]
    return vals.transpose(0, 1, 3, 2).reshape(g * 512, n)


def pack4(w):
    words, scales = pack_weight(w, "e2m1")
    return words.reshape(words.shape[0], 128, -1), scales


def unpack4(words, scales):
    return unpack_weight(words.reshape(words.shape[0], 128, -1, 2), scales, "e2m1")


B, S, K, N = 2, 128, 2048, 8192


def setup_inputs():
    s = mx_kscale(K)
    x = bf(np.random.standard_normal((B, S, K)) * s)
    w = np.random.standard_normal((K, N)) * 0.022 / s[:, None]
    w_words, w_scales = pack4(w)
    bias = bf(np.random.standard_normal(N))
    return {"x": x, "w_words": w_words, "w_scales": w_scales, "bias": bias}


def reference(x, w_words, w_scales, bias):
    w = unpack4(w_words, w_scales)
    return (mxq(f64(x), 2, "e4m3") @ w) + f64(bias)

@@ -1,0 +1,192 @@
+from contextlib import ExitStack
+
+import concourse.mybir as mybir
+from concourse.masks import make_identity
+
+BF16 = mybir.dt.bfloat16
+F32 = mybir.dt.float32
+I32 = mybir.dt.int32
+U8 = mybir.dt.uint8
+U32 = mybir.dt.uint32
+FP8X4 = mybir.dt.float8_e4m3fn_x4
+FP4X4 = mybir.dt.float4_e2m1fn_x4
+
+P = 128
+K = 2048
+N = 8192
+M_TILES = 2
+PASSES = K // 512
+CHUNK = 512
+N_CHUNKS = N // CHUNK
+
+FLOPS = 2 * M_TILES * P * K * N
+
+SCALE_GROUPS = [(0, 2048), (2048, 4096), (4096, 6144), (6144, 8192)]
+WORD_PIECES = [(0, 1024), (1024, 2048), (2048, 4096), (4096, 6144), (6144, 8192)]
+STORE_PIECES = [(0, 2048), (2048, 4096), (4096, 6144), (6144, 7168), (7168, 8192)]
+G_PER_SCALE_DMA = 4
+
+
+def find_piece(pieces, col):
+    for i, (lo, hi) in enumerate(pieces):
+        if lo <= col < hi:
+            return i, lo
+    raise ValueError("column outside every piece")
+
+
+def tile_quantizedlinear_kernel(tc, x, w_words, w_scales, bias, out):
+    nc = tc.nc
+    with ExitStack() as ctx:
+        keep = ctx.enter_context(tc.tile_pool(name="keep", bufs=1))
+        psum = ctx.enter_context(tc.psum_pool(name="psum", bufs=8))
+        ctx.enter_context(tc.manual_schedule())
+
+        ident_b = keep.tile([P, P], BF16, name="ident_b")
+        make_identity(nc, ident_b[:])
+        ident_f = keep.tile([P, P], F32, name="ident_f")
+        make_identity(nc, ident_f[:])
+
+        bias_rows = keep.tile([P, CHUNK], BF16, name="bias_rows")
+        nc.vector.memset(bias_rows[:], 0.0)
+
+        planes = []
+        for j, (lo, hi) in enumerate(SCALE_GROUPS):
+            planes.append(keep.tile([P, PASSES, hi - lo], U8, name="plane%d" % j, align_bytes=64))
+
+        def zero_plane(j):
+            nc.vector.memset(planes[j][:].rearrange("p g n -> p (g n)").bitcast(I32), 0)
+
+        zero_plane(0)
+
+        x_sb = []
+        for m in range(M_TILES):
+            xt = keep.tile([P, K], BF16, name="x%d" % m)
+            nc.sync.dma_start(out=xt[:], in_=x[m])
+            x_sb.append(xt)
+
+        nc.scalar.dma_start(out=bias_rows[0:16, :], in_=bias.rearrange("(j c) -> j c", c=CHUNK))
+
+        scale_rows = w_scales.rearrange("g (h q) n -> h q g n", h=2)
+        words_by_p = w_words.rearrange("g p b -> p g b")
+
+        def load_scales(j):
+            lo, hi = SCALE_GROUPS[j]
+            for g0 in range(0, PASSES, G_PER_SCALE_DMA):
+                g1 = g0 + G_PER_SCALE_DMA
+                for b in range(2):
+                    for r in range(4):
+                        nc.sync.dma_start(
+                            out=planes[j][32 * b + r : P : 64, g0:g1, :].bitcast(I32),
+                            in_=scale_rows[:, 4 * b + r, g0:g1, lo:hi].bitcast(I32),
+                        )
+
+        words = []
+
+        def load_words(i):
+            lo, hi = WORD_PIECES[i]
+            wt = keep.tile([P, PASSES, 2 * (hi - lo)], U8, name="w%d" % i, align_bytes=64)
+            nc.sync.dma_start(out=wt[:].bitcast(I32), in_=words_by_p[:, :, 2 * lo : 2 * hi].bitcast(I32))
+            words.append(wt)
+
+        bias_bc = keep.tile([P, N], BF16, name="bias_bc")
+
+        def spread_bias(t):
+            bp = psum.tile([P, 2 * CHUNK], BF16, tag="bank", name="bp")
+            for h in range(2):
+                j = 2 * t + h
+                nc.tensor.matmul(
+                    bp[:, h * CHUNK : (h + 1) * CHUNK],
+                    lhsT=ident_b[:, j : j + 1].to_broadcast([P, P]),
+                    rhs=bias_rows[:],
+                    start=True,
+                    stop=True,
+                )
+            nc.scalar.copy(out=bias_bc[:, 2 * t * CHUNK : 2 * (t + 1) * CHUNK], in_=bp[:])
+
+        grouped = keep.tile([P, M_TILES * PASSES * P * 4], BF16, name="grouped", align_bytes=64)
+        grouped_w = grouped[:].bitcast(F32)
+        xq = keep.tile([P, M_TILES * PASSES * P], U32, name="xq", align_bytes=64)
+        xs = keep.tile([P, M_TILES * PASSES * P], U8, name="xs", align_bytes=64)
+
+        def transpose_x(m):
+            xw = x_sb[m][:].bitcast(F32)
+            for half in range(2):
+                tp = psum.tile([P, 2, 2, P], F32, tag="bank", name="tp")
+                for a in range(2):
+                    g = 2 * half + a
+                    for u in range(2):
+                        nc.tensor.transpose(tp[:, a, u, :], xw[:, 256 * g + u : 256 * (g + 1) : 2], ident_f[:])
+                unit = m * PASSES + 2 * half
+                dst = grouped_w[:, unit * 2 * P : (unit + 2) * 2 * P].rearrange("p (a r u) -> p a r u", a=2, u=2)
+                src = tp[:].rearrange("p a u r -> p a r u")
+                if half == 0:
+                    nc.vector.tensor_copy(out=dst, in_=src)
+                else:
+                    nc.scalar.copy(out=dst, in_=src)
+
+        def quantise_x(m):
+            w = PASSES * P
+            nc.vector.quantize_mx(
+                out=xq[:, m * w : (m + 1) * w].bitcast(FP8X4),
+                scales=xs[:, m * w : (m + 1) * w],
+                in_=grouped[:, m * 4 * w : (m + 1) * 4 * w],
+            )
+
+        next_piece = 0
+        for j, (lo, hi) in enumerate(SCALE_GROUPS):
+            if j > 0:
+                break
+            load_scales(j)
+            while next_piece < len(WORD_PIECES) and WORD_PIECES[next_piece][1] <= hi:
+                load_words(next_piece)
+                next_piece += 1
+
+        spread_bias(0)
+        spread_bias(1)
+        transpose_x(0)
+        transpose_x(1)
+        quantise_x(0)
+        quantise_x(1)
+
+        for j in range(1, len(SCALE_GROUPS)):
+            zero_plane(j)
+            load_scales(j)
+            while next_piece < len(WORD_PIECES) and WORD_PIECES[next_piece][1] <= SCALE_GROUPS[j][1]:
+                load_words(next_piece)
+                next_piece += 1
+
+        for t in range(2, N_CHUNKS // 2):
+            spread_bias(t)
+
+        o_tiles = {}
+        for c in range(N_CHUNKS):
+            col = c * CHUNK
+            jg, glo = find_piece(SCALE_GROUPS, col)
+            iw, wlo = find_piece(WORD_PIECES, col)
+            si, slo = find_piece(STORE_PIECES, col)
+            shi = STORE_PIECES[si][1]
+            for m in range(M_TILES):
+                acc = psum.tile([P, CHUNK], F32, tag="bank", name="acc")
+                for g in range(PASSES):
+                    unit = m * PASSES + g
+                    nc.tensor.matmul_mx(
+                        out=acc[:],
+                        lhsT=xq[:, unit * P : (unit + 1) * P].bitcast(FP8X4),
+                        lhsT_scale=xs[:, unit * P : (unit + 1) * P],
+                        rhs=words[iw][:, g, 2 * (col - wlo) : 2 * (col - wlo + CHUNK)].bitcast(FP4X4),
+                        rhs_scale=planes[jg][:, g, col - glo : col - glo + CHUNK],
+                        start=(g == 0),
+                        stop=(g == PASSES - 1),
+                    )
+                if (si, m) not in o_tiles:
+                    o_tiles[(si, m)] = keep.tile([P, shi - slo], F32, name="o%d_%d" % (si, m))
+                ot = o_tiles[(si, m)]
+                nc.vector.tensor_tensor(
+                    out=ot[:, col - slo : col - slo + CHUNK],
+                    in0=acc[:],
+                    in1=bias_bc[:, col : col + CHUNK],
+                    op=mybir.AluOpType.add,
+                )
+            if col + CHUNK == shi:
+                for m in range(M_TILES):
+                    nc.sync.dma_start(out=out[m, :, slo:shi], in_=o_tiles[(si, m)][:])

@@ -23,8 +23,9 @@ FLOPS = 2 * M_TILES * P * K * N
 
 SCALE_GROUPS = [(0, 2048), (2048, 4096), (4096, 6144), (6144, 8192)]
 WORD_PIECES = [(0, 1024), (1024, 2048), (2048, 4096), (4096, 6144), (6144, 8192)]
-STORE_PIECES = [(0, 2048), (2048, 4096), (4096, 6144), (6144, 7168), (7168, 8192)]
-G_PER_SCALE_DMA = 4
+STORE_PIECES = [(0, 2048), (2048, 4096), (4096, 6144), (6144, 7168), (7168, 7680), (7680, 8192)]
+SYNC_LOADS = [("s", 0), ("w", 0), ("w", 1), ("w", 2), ("w", 3), ("w", 4)]
+GPSIMD_SCALES = [1, 2, 3]
 
 
 def find_piece(pieces, col):
@@ -41,22 +42,19 @@ def tile_quantizedlinear_kernel(tc, x, w_words, w_scales, bias, out):
         psum = ctx.enter_context(tc.psum_pool(name="psum", bufs=8))
         ctx.enter_context(tc.manual_schedule())
 
-        ident_b = keep.tile([P, P], BF16, name="ident_b")
-        make_identity(nc, ident_b[:])
         ident_f = keep.tile([P, P], F32, name="ident_f")
         make_identity(nc, ident_f[:])
 
         bias_rows = keep.tile([P, CHUNK], BF16, name="bias_rows")
         nc.vector.memset(bias_rows[:], 0.0)
+        ident_b = keep.tile([P, P], BF16, name="ident_b")
+        nc.vector.tensor_copy(out=ident_b[:], in_=ident_f[:])
 
         planes = []
         for j, (lo, hi) in enumerate(SCALE_GROUPS):
-            planes.append(keep.tile([P, PASSES, hi - lo], U8, name="plane%d" % j, align_bytes=64))
-
-        def zero_plane(j):
-            nc.vector.memset(planes[j][:].rearrange("p g n -> p (g n)").bitcast(I32), 0)
-
-        zero_plane(0)
+            plane = keep.tile([P, PASSES, hi - lo], U8, name="plane%d" % j, align_bytes=64)
+            nc.vector.memset(plane[:].rearrange("p g n -> p (g n)").bitcast(I32), 0)
+            planes.append(plane)
 
         x_sb = []
         for m in range(M_TILES):
@@ -69,24 +67,30 @@ def tile_quantizedlinear_kernel(tc, x, w_words, w_scales, bias, out):
         scale_rows = w_scales.rearrange("g (h q) n -> h q g n", h=2)
         words_by_p = w_words.rearrange("g p b -> p g b")
 
-        def load_scales(j):
+        def load_scales(j, queue, view):
             lo, hi = SCALE_GROUPS[j]
-            for g0 in range(0, PASSES, G_PER_SCALE_DMA):
-                g1 = g0 + G_PER_SCALE_DMA
-                for b in range(2):
-                    for r in range(4):
-                        nc.sync.dma_start(
-                            out=planes[j][32 * b + r : P : 64, g0:g1, :].bitcast(I32),
-                            in_=scale_rows[:, 4 * b + r, g0:g1, lo:hi].bitcast(I32),
-                        )
+            for b in range(2):
+                for r in range(4):
+                    queue.dma_start(
+                        out=planes[j][32 * b + r : P : 64, :, :].bitcast(view),
+                        in_=scale_rows[:, 4 * b + r, :, lo:hi].bitcast(view),
+                    )
 
-        words = []
+        words = {}
 
         def load_words(i):
             lo, hi = WORD_PIECES[i]
             wt = keep.tile([P, PASSES, 2 * (hi - lo)], U8, name="w%d" % i, align_bytes=64)
             nc.sync.dma_start(out=wt[:].bitcast(I32), in_=words_by_p[:, :, 2 * lo : 2 * hi].bitcast(I32))
-            words.append(wt)
+            words[i] = wt
+
+        for kind, i in SYNC_LOADS:
+            if kind == "s":
+                load_scales(i, nc.sync, I32)
+            else:
+                load_words(i)
+        for j in GPSIMD_SCALES:
+            load_scales(j, nc.gpsimd, F32)
 
         bias_bc = keep.tile([P, N], BF16, name="bias_bc")
 
@@ -132,29 +136,12 @@ def tile_quantizedlinear_kernel(tc, x, w_words, w_scales, bias, out):
                 in_=grouped[:, m * 4 * w : (m + 1) * 4 * w],
             )
 
-        next_piece = 0
-        for j, (lo, hi) in enumerate(SCALE_GROUPS):
-            if j > 0:
-                break
-            load_scales(j)
-            while next_piece < len(WORD_PIECES) and WORD_PIECES[next_piece][1] <= hi:
-                load_words(next_piece)
-                next_piece += 1
-
         spread_bias(0)
         spread_bias(1)
         transpose_x(0)
         transpose_x(1)
         quantise_x(0)
         quantise_x(1)
-
-        for j in range(1, len(SCALE_GROUPS)):
-            zero_plane(j)
-            load_scales(j)
-            while next_piece < len(WORD_PIECES) and WORD_PIECES[next_piece][1] <= SCALE_GROUPS[j][1]:
-                load_words(next_piece)
-                next_piece += 1
-
         for t in range(2, N_CHUNKS // 2):
             spread_bias(t)
 

@@ -23,7 +23,17 @@ FLOPS = 2 * M_TILES * P * K * N
 
 SCALE_GROUPS = [(0, 2048), (2048, 4096), (4096, 6144), (6144, 8192)]
 WORD_PIECES = [(0, 1024), (1024, 2048), (2048, 4096), (4096, 6144), (6144, 8192)]
-STORE_PIECES = [(0, 2048), (2048, 4096), (4096, 6144), (6144, 7168), (7168, 7680), (7680, 8192)]
+STORE_PIECES = [
+    (0, 1024),
+    (1024, 2048),
+    (2048, 3072),
+    (3072, 4096),
+    (4096, 5120),
+    (5120, 6144),
+    (6144, 7168),
+    (7168, 7680),
+    (7680, 8192),
+]
 SYNC_LOADS = [("s", 0), ("w", 0), ("w", 1), ("w", 2), ("w", 3), ("w", 4)]
 GPSIMD_SCALES = [1, 2, 3]
 
@@ -176,4 +186,4 @@ def tile_quantizedlinear_kernel(tc, x, w_words, w_scales, bias, out):
                 )
             if col + CHUNK == shi:
                 for m in range(M_TILES):
-                    nc.sync.dma_start(out=out[m, :, slo:shi], in_=o_tiles[(si, m)][:])
+                    nc.scalar.dma_start(out=out[m, :, slo:shi], in_=o_tiles[(si, m)][:])

@@ -22,7 +22,16 @@ N_CHUNKS = N // CHUNK
 FLOPS = 2 * M_TILES * P * K * N
 
 SCALE_GROUPS = [(0, 2048), (2048, 4096), (4096, 6144), (6144, 8192)]
-WORD_PIECES = [(0, 1024), (1024, 2048), (2048, 4096), (4096, 6144), (6144, 8192)]
+WORD_PIECES = [
+    (0, 1024),
+    (1024, 2048),
+    (2048, 3072),
+    (3072, 4096),
+    (4096, 5120),
+    (5120, 6144),
+    (6144, 7168),
+    (7168, 8192),
+]
 STORE_PIECES = [
     (0, 1024),
     (1024, 2048),
@@ -34,7 +43,7 @@ STORE_PIECES = [
     (7168, 7680),
     (7680, 8192),
 ]
-SYNC_LOADS = [("s", 0), ("w", 0), ("w", 1), ("w", 2), ("w", 3), ("w", 4)]
+SYNC_LOADS = [("s", 0), ("w", 0), ("w", 1), ("w", 2), ("w", 3), ("w", 4), ("w", 5), ("w", 6), ("w", 7)]
 GPSIMD_SCALES = [1, 2, 3]
 
 

@@ -18,19 +18,22 @@ M_TILES = 2
 PASSES = K // 512
 CHUNK = 512
 N_CHUNKS = N // CHUNK
+BIAS_ROWS = N // CHUNK
 
 FLOPS = 2 * M_TILES * P * K * N
 
 SCALE_GROUPS = [(0, 2048), (2048, 4096), (4096, 6144), (6144, 8192)]
 WORD_PIECES = [
-    (0, 1024),
+    (0, 512),
+    (512, 1024),
     (1024, 2048),
     (2048, 3072),
     (3072, 4096),
     (4096, 5120),
     (5120, 6144),
     (6144, 7168),
-    (7168, 8192),
+    (7168, 7680),
+    (7680, 8192),
 ]
 STORE_PIECES = [
     (0, 1024),
@@ -43,8 +46,10 @@ STORE_PIECES = [
     (7168, 7680),
     (7680, 8192),
 ]
-SYNC_LOADS = [("s", 0), ("w", 0), ("w", 1), ("w", 2), ("w", 3), ("w", 4), ("w", 5), ("w", 6), ("w", 7)]
 GPSIMD_SCALES = [1, 2, 3]
+ZERO_AFTER_CHUNK = {2: 1, 3: 4}
+N_DUMMIES = 4
+TAIL_N = 128
 
 
 def find_piece(pieces, col):
@@ -61,27 +66,34 @@ def tile_quantizedlinear_kernel(tc, x, w_words, w_scales, bias, out):
         psum = ctx.enter_context(tc.psum_pool(name="psum", bufs=8))
         ctx.enter_context(tc.manual_schedule())
 
-        ident_f = keep.tile([P, P], F32, name="ident_f")
-        make_identity(nc, ident_f[:])
-
         bias_rows = keep.tile([P, CHUNK], BF16, name="bias_rows")
-        nc.vector.memset(bias_rows[:], 0.0)
-        ident_b = keep.tile([P, P], BF16, name="ident_b")
-        nc.vector.tensor_copy(out=ident_b[:], in_=ident_f[:])
-
-        planes = []
-        for j, (lo, hi) in enumerate(SCALE_GROUPS):
-            plane = keep.tile([P, PASSES, hi - lo], U8, name="plane%d" % j, align_bytes=64)
-            nc.vector.memset(plane[:].rearrange("p g n -> p (g n)").bitcast(I32), 0)
-            planes.append(plane)
-
+        nc.scalar.dma_start(
+            out=bias_rows[:],
+            in_=bias.rearrange("(j c) -> j c", c=CHUNK).unsqueeze(0).to_broadcast([P // BIAS_ROWS, BIAS_ROWS, CHUNK]),
+        )
         x_sb = []
         for m in range(M_TILES):
             xt = keep.tile([P, K], BF16, name="x%d" % m)
             nc.sync.dma_start(out=xt[:], in_=x[m])
             x_sb.append(xt)
 
-        nc.scalar.dma_start(out=bias_rows[0:16, :], in_=bias.rearrange("(j c) -> j c", c=CHUNK))
+        ident_f = keep.tile([P, P], F32, name="ident_f")
+        make_identity(nc, ident_f[:])
+
+        warm = keep.tile([P, CHUNK], BF16, name="warm")
+        nc.vector.memset(warm[:], 0.0)
+        ident_b = keep.tile([P, P], BF16, name="ident_b")
+        nc.vector.tensor_copy(out=ident_b[:], in_=ident_f[:])
+
+        planes = []
+        for j, (lo, hi) in enumerate(SCALE_GROUPS):
+            planes.append(keep.tile([P, PASSES, hi - lo], U8, name="plane%d" % j, align_bytes=64))
+
+        def zero_plane(j):
+            nc.vector.memset(planes[j][:].rearrange("p g n -> p (g n)").bitcast(I32), 0)
+
+        zero_plane(0)
+        zero_plane(1)
 
         scale_rows = w_scales.rearrange("g (h q) n -> h q g n", h=2)
         words_by_p = w_words.rearrange("g p b -> p g b")
@@ -95,21 +107,17 @@ def tile_quantizedlinear_kernel(tc, x, w_words, w_scales, bias, out):
                         in_=scale_rows[:, 4 * b + r, :, lo:hi].bitcast(view),
                     )
 
-        words = {}
-
-        def load_words(i):
-            lo, hi = WORD_PIECES[i]
+        load_scales(0, nc.sync, I32)
+        words = []
+        for i, (lo, hi) in enumerate(WORD_PIECES):
             wt = keep.tile([P, PASSES, 2 * (hi - lo)], U8, name="w%d" % i, align_bytes=64)
             nc.sync.dma_start(out=wt[:].bitcast(I32), in_=words_by_p[:, :, 2 * lo : 2 * hi].bitcast(I32))
-            words[i] = wt
+            words.append(wt)
+        load_scales(1, nc.gpsimd, F32)
 
-        for kind, i in SYNC_LOADS:
-            if kind == "s":
-                load_scales(i, nc.sync, I32)
-            else:
-                load_words(i)
-        for j in GPSIMD_SCALES:
-            load_scales(j, nc.gpsimd, F32)
+        dummy = psum.tile([P, CHUNK], F32, tag="bank", name="dummy")
+        for i in range(N_DUMMIES):
+            nc.tensor.matmul(dummy[:], lhsT=warm[:, 0:P], rhs=warm[:], start=True, stop=True)
 
         bias_bc = keep.tile([P, N], BF16, name="bias_bc")
 
@@ -131,21 +139,20 @@ def tile_quantizedlinear_kernel(tc, x, w_words, w_scales, bias, out):
         xq = keep.tile([P, M_TILES * PASSES * P], U32, name="xq", align_bytes=64)
         xs = keep.tile([P, M_TILES * PASSES * P], U8, name="xs", align_bytes=64)
 
-        def transpose_x(m):
+        def transpose_x(m, half):
             xw = x_sb[m][:].bitcast(F32)
-            for half in range(2):
-                tp = psum.tile([P, 2, 2, P], F32, tag="bank", name="tp")
-                for a in range(2):
-                    g = 2 * half + a
-                    for u in range(2):
-                        nc.tensor.transpose(tp[:, a, u, :], xw[:, 256 * g + u : 256 * (g + 1) : 2], ident_f[:])
-                unit = m * PASSES + 2 * half
-                dst = grouped_w[:, unit * 2 * P : (unit + 2) * 2 * P].rearrange("p (a r u) -> p a r u", a=2, u=2)
-                src = tp[:].rearrange("p a u r -> p a r u")
-                if half == 0:
-                    nc.vector.tensor_copy(out=dst, in_=src)
-                else:
-                    nc.scalar.copy(out=dst, in_=src)
+            tp = psum.tile([P, 2, 2, P], F32, tag="bank", name="tp")
+            for a in range(2):
+                g = 2 * half + a
+                for u in range(2):
+                    nc.tensor.transpose(tp[:, a, u, :], xw[:, 256 * g + u : 256 * (g + 1) : 2], ident_f[:])
+            unit = m * PASSES + 2 * half
+            dst = grouped_w[:, unit * 2 * P : (unit + 2) * 2 * P].rearrange("p (a r u) -> p a r u", a=2, u=2)
+            src = tp[:].rearrange("p a u r -> p a r u")
+            if half == 0:
+                nc.vector.tensor_copy(out=dst, in_=src)
+            else:
+                nc.scalar.copy(out=dst, in_=src)
 
         def quantise_x(m):
             w = PASSES * P
@@ -157,42 +164,64 @@ def tile_quantizedlinear_kernel(tc, x, w_words, w_scales, bias, out):
 
         spread_bias(0)
         spread_bias(1)
-        transpose_x(0)
-        transpose_x(1)
+        transpose_x(0, 0)
+        spread_bias(2)
+        transpose_x(0, 1)
+        transpose_x(1, 0)
+        spread_bias(3)
+        transpose_x(1, 1)
         quantise_x(0)
         quantise_x(1)
-        for t in range(2, N_CHUNKS // 2):
+        for t in range(4, N_CHUNKS // 2):
             spread_bias(t)
+
+        def product(c, m, lo, width, ot, slo):
+            jg, glo = find_piece(SCALE_GROUPS, lo)
+            iw, wlo = find_piece(WORD_PIECES, lo)
+            acc = psum.tile([P, width], F32, tag="bank", name="acc")
+            for g in range(PASSES):
+                unit = m * PASSES + g
+                nc.tensor.matmul_mx(
+                    out=acc[:],
+                    lhsT=xq[:, unit * P : (unit + 1) * P].bitcast(FP8X4),
+                    lhsT_scale=xs[:, unit * P : (unit + 1) * P],
+                    rhs=words[iw][:, g, 2 * (lo - wlo) : 2 * (lo - wlo + width)].bitcast(FP4X4),
+                    rhs_scale=planes[jg][:, g, lo - glo : lo - glo + width],
+                    start=(g == 0),
+                    stop=(g == PASSES - 1),
+                )
+            nc.vector.tensor_tensor(
+                out=ot[:, lo - slo : lo - slo + width],
+                in0=acc[:],
+                in1=bias_bc[:, lo : lo + width],
+                op=mybir.AluOpType.add,
+            )
 
         o_tiles = {}
         for c in range(N_CHUNKS):
             col = c * CHUNK
-            jg, glo = find_piece(SCALE_GROUPS, col)
-            iw, wlo = find_piece(WORD_PIECES, col)
             si, slo = find_piece(STORE_PIECES, col)
             shi = STORE_PIECES[si][1]
+            last = c == N_CHUNKS - 1
             for m in range(M_TILES):
-                acc = psum.tile([P, CHUNK], F32, tag="bank", name="acc")
-                for g in range(PASSES):
-                    unit = m * PASSES + g
-                    nc.tensor.matmul_mx(
-                        out=acc[:],
-                        lhsT=xq[:, unit * P : (unit + 1) * P].bitcast(FP8X4),
-                        lhsT_scale=xs[:, unit * P : (unit + 1) * P],
-                        rhs=words[iw][:, g, 2 * (col - wlo) : 2 * (col - wlo + CHUNK)].bitcast(FP4X4),
-                        rhs_scale=planes[jg][:, g, col - glo : col - glo + CHUNK],
-                        start=(g == 0),
-                        stop=(g == PASSES - 1),
-                    )
                 if (si, m) not in o_tiles:
                     o_tiles[(si, m)] = keep.tile([P, shi - slo], F32, name="o%d_%d" % (si, m))
                 ot = o_tiles[(si, m)]
-                nc.vector.tensor_tensor(
-                    out=ot[:, col - slo : col - slo + CHUNK],
-                    in0=acc[:],
-                    in1=bias_bc[:, col : col + CHUNK],
-                    op=mybir.AluOpType.add,
-                )
-            if col + CHUNK == shi:
+                if last and m == M_TILES - 1:
+                    for q in range(CHUNK // TAIL_N):
+                        product(c, m, col + q * TAIL_N, TAIL_N, ot, slo)
+                        if q % 2 == 1:
+                            a = col + (q - 1) * TAIL_N
+                            b = col + (q + 1) * TAIL_N
+                            nc.scalar.dma_start(out=out[m, :, a:b], in_=ot[:, a - slo : b - slo])
+                else:
+                    product(c, m, col, CHUNK, ot, slo)
+                    if last:
+                        nc.scalar.dma_start(out=out[m, :, slo:shi], in_=ot[:])
+            if col + CHUNK == shi and not last:
                 for m in range(M_TILES):
                     nc.scalar.dma_start(out=out[m, :, slo:shi], in_=o_tiles[(si, m)][:])
+            for j in GPSIMD_SCALES:
+                if ZERO_AFTER_CHUNK.get(j) == c:
+                    zero_plane(j)
+                    load_scales(j, nc.gpsimd, F32)

@@ -18,14 +18,12 @@ M_TILES = 2
 PASSES = K // 512
 CHUNK = 512
 N_CHUNKS = N // CHUNK
-BIAS_ROWS = N // CHUNK
 
 FLOPS = 2 * M_TILES * P * K * N
 
 SCALE_GROUPS = [(0, 2048), (2048, 4096), (4096, 6144), (6144, 8192)]
 WORD_PIECES = [
-    (0, 512),
-    (512, 1024),
+    (0, 1024),
     (1024, 2048),
     (2048, 3072),
     (3072, 4096),
@@ -46,10 +44,9 @@ STORE_PIECES = [
     (7168, 7680),
     (7680, 8192),
 ]
-GPSIMD_SCALES = [1, 2, 3]
-ZERO_AFTER_CHUNK = {2: 1, 3: 4}
-N_DUMMIES = 4
+SYNC_LOADS = [("s", 0), ("w", 0), ("w", 1), ("w", 2), ("w", 3), ("w", 4), ("w", 5), ("w", 6), ("w", 7), ("w", 8)]
 TAIL_N = 128
+GPSIMD_SCALES = [1, 2, 3]
 
 
 def find_piece(pieces, col):
@@ -66,34 +63,27 @@ def tile_quantizedlinear_kernel(tc, x, w_words, w_scales, bias, out):
         psum = ctx.enter_context(tc.psum_pool(name="psum", bufs=8))
         ctx.enter_context(tc.manual_schedule())
 
+        ident_f = keep.tile([P, P], F32, name="ident_f")
+        make_identity(nc, ident_f[:])
+
         bias_rows = keep.tile([P, CHUNK], BF16, name="bias_rows")
-        nc.scalar.dma_start(
-            out=bias_rows[:],
-            in_=bias.rearrange("(j c) -> j c", c=CHUNK).unsqueeze(0).to_broadcast([P // BIAS_ROWS, BIAS_ROWS, CHUNK]),
-        )
+        nc.vector.memset(bias_rows[:], 0.0)
+        ident_b = keep.tile([P, P], BF16, name="ident_b")
+        nc.vector.tensor_copy(out=ident_b[:], in_=ident_f[:])
+
+        planes = []
+        for j, (lo, hi) in enumerate(SCALE_GROUPS):
+            plane = keep.tile([P, PASSES, hi - lo], U8, name="plane%d" % j, align_bytes=64)
+            nc.vector.memset(plane[:].rearrange("p g n -> p (g n)").bitcast(I32), 0)
+            planes.append(plane)
+
         x_sb = []
         for m in range(M_TILES):
             xt = keep.tile([P, K], BF16, name="x%d" % m)
             nc.sync.dma_start(out=xt[:], in_=x[m])
             x_sb.append(xt)
 
-        ident_f = keep.tile([P, P], F32, name="ident_f")
-        make_identity(nc, ident_f[:])
-
-        warm = keep.tile([P, CHUNK], BF16, name="warm")
-        nc.vector.memset(warm[:], 0.0)
-        ident_b = keep.tile([P, P], BF16, name="ident_b")
-        nc.vector.tensor_copy(out=ident_b[:], in_=ident_f[:])
-
-        planes = []
-        for j, (lo, hi) in enumerate(SCALE_GROUPS):
-            planes.append(keep.tile([P, PASSES, hi - lo], U8, name="plane%d" % j, align_bytes=64))
-
-        def zero_plane(j):
-            nc.vector.memset(planes[j][:].rearrange("p g n -> p (g n)").bitcast(I32), 0)
-
-        zero_plane(0)
-        zero_plane(1)
+        nc.scalar.dma_start(out=bias_rows[0:16, :], in_=bias.rearrange("(j c) -> j c", c=CHUNK))
 
         scale_rows = w_scales.rearrange("g (h q) n -> h q g n", h=2)
         words_by_p = w_words.rearrange("g p b -> p g b")
@@ -107,17 +97,21 @@ def tile_quantizedlinear_kernel(tc, x, w_words, w_scales, bias, out):
                         in_=scale_rows[:, 4 * b + r, :, lo:hi].bitcast(view),
                     )
 
-        load_scales(0, nc.sync, I32)
-        words = []
-        for i, (lo, hi) in enumerate(WORD_PIECES):
+        words = {}
+
+        def load_words(i):
+            lo, hi = WORD_PIECES[i]
             wt = keep.tile([P, PASSES, 2 * (hi - lo)], U8, name="w%d" % i, align_bytes=64)
             nc.sync.dma_start(out=wt[:].bitcast(I32), in_=words_by_p[:, :, 2 * lo : 2 * hi].bitcast(I32))
-            words.append(wt)
-        load_scales(1, nc.gpsimd, F32)
+            words[i] = wt
 
-        dummy = psum.tile([P, CHUNK], F32, tag="bank", name="dummy")
-        for i in range(N_DUMMIES):
-            nc.tensor.matmul(dummy[:], lhsT=warm[:, 0:P], rhs=warm[:], start=True, stop=True)
+        for kind, i in SYNC_LOADS:
+            if kind == "s":
+                load_scales(i, nc.sync, I32)
+            else:
+                load_words(i)
+        for j in GPSIMD_SCALES:
+            load_scales(j, nc.gpsimd, F32)
 
         bias_bc = keep.tile([P, N], BF16, name="bias_bc")
 
@@ -139,20 +133,21 @@ def tile_quantizedlinear_kernel(tc, x, w_words, w_scales, bias, out):
         xq = keep.tile([P, M_TILES * PASSES * P], U32, name="xq", align_bytes=64)
         xs = keep.tile([P, M_TILES * PASSES * P], U8, name="xs", align_bytes=64)
 
-        def transpose_x(m, half):
+        def transpose_x(m):
             xw = x_sb[m][:].bitcast(F32)
-            tp = psum.tile([P, 2, 2, P], F32, tag="bank", name="tp")
-            for a in range(2):
-                g = 2 * half + a
-                for u in range(2):
-                    nc.tensor.transpose(tp[:, a, u, :], xw[:, 256 * g + u : 256 * (g + 1) : 2], ident_f[:])
-            unit = m * PASSES + 2 * half
-            dst = grouped_w[:, unit * 2 * P : (unit + 2) * 2 * P].rearrange("p (a r u) -> p a r u", a=2, u=2)
-            src = tp[:].rearrange("p a u r -> p a r u")
-            if half == 0:
-                nc.vector.tensor_copy(out=dst, in_=src)
-            else:
-                nc.scalar.copy(out=dst, in_=src)
+            for half in range(2):
+                tp = psum.tile([P, 2, 2, P], F32, tag="bank", name="tp")
+                for a in range(2):
+                    g = 2 * half + a
+                    for u in range(2):
+                        nc.tensor.transpose(tp[:, a, u, :], xw[:, 256 * g + u : 256 * (g + 1) : 2], ident_f[:])
+                unit = m * PASSES + 2 * half
+                dst = grouped_w[:, unit * 2 * P : (unit + 2) * 2 * P].rearrange("p (a r u) -> p a r u", a=2, u=2)
+                src = tp[:].rearrange("p a u r -> p a r u")
+                if half == 0:
+                    nc.vector.tensor_copy(out=dst, in_=src)
+                else:
+                    nc.scalar.copy(out=dst, in_=src)
 
         def quantise_x(m):
             w = PASSES * P
@@ -164,18 +159,14 @@ def tile_quantizedlinear_kernel(tc, x, w_words, w_scales, bias, out):
 
         spread_bias(0)
         spread_bias(1)
-        transpose_x(0, 0)
-        spread_bias(2)
-        transpose_x(0, 1)
-        transpose_x(1, 0)
-        spread_bias(3)
-        transpose_x(1, 1)
+        transpose_x(0)
+        transpose_x(1)
         quantise_x(0)
         quantise_x(1)
-        for t in range(4, N_CHUNKS // 2):
+        for t in range(2, N_CHUNKS // 2):
             spread_bias(t)
 
-        def product(c, m, lo, width, ot, slo):
+        def product(m, lo, width, ot, slo):
             jg, glo = find_piece(SCALE_GROUPS, lo)
             iw, wlo = find_piece(WORD_PIECES, lo)
             acc = psum.tile([P, width], F32, tag="bank", name="acc")
@@ -209,19 +200,15 @@ def tile_quantizedlinear_kernel(tc, x, w_words, w_scales, bias, out):
                 ot = o_tiles[(si, m)]
                 if last and m == M_TILES - 1:
                     for q in range(CHUNK // TAIL_N):
-                        product(c, m, col + q * TAIL_N, TAIL_N, ot, slo)
+                        product(m, col + q * TAIL_N, TAIL_N, ot, slo)
                         if q % 2 == 1:
                             a = col + (q - 1) * TAIL_N
                             b = col + (q + 1) * TAIL_N
                             nc.scalar.dma_start(out=out[m, :, a:b], in_=ot[:, a - slo : b - slo])
                 else:
-                    product(c, m, col, CHUNK, ot, slo)
+                    product(m, col, CHUNK, ot, slo)
                     if last:
                         nc.scalar.dma_start(out=out[m, :, slo:shi], in_=ot[:])
             if col + CHUNK == shi and not last:
                 for m in range(M_TILES):
                     nc.scalar.dma_start(out=out[m, :, slo:shi], in_=o_tiles[(si, m)][:])
-            for j in GPSIMD_SCALES:
-                if ZERO_AFTER_CHUNK.get(j) == c:
-                    zero_plane(j)
-                    load_scales(j, nc.gpsimd, F32)

@@ -18,12 +18,14 @@ M_TILES = 2
 PASSES = K // 512
 CHUNK = 512
 N_CHUNKS = N // CHUNK
+BIAS_ROWS = N // CHUNK
 
 FLOPS = 2 * M_TILES * P * K * N
 
 SCALE_GROUPS = [(0, 2048), (2048, 4096), (4096, 6144), (6144, 8192)]
 WORD_PIECES = [
-    (0, 1024),
+    (0, 512),
+    (512, 1024),
     (1024, 2048),
     (2048, 3072),
     (3072, 4096),
@@ -44,9 +46,10 @@ STORE_PIECES = [
     (7168, 7680),
     (7680, 8192),
 ]
-SYNC_LOADS = [("s", 0), ("w", 0), ("w", 1), ("w", 2), ("w", 3), ("w", 4), ("w", 5), ("w", 6), ("w", 7), ("w", 8)]
-TAIL_N = 128
 GPSIMD_SCALES = [1, 2, 3]
+ZERO_AFTER_CHUNK = {3: 1}
+N_DUMMIES = 4
+TAIL_N = 128
 
 
 def find_piece(pieces, col):
@@ -63,27 +66,33 @@ def tile_quantizedlinear_kernel(tc, x, w_words, w_scales, bias, out):
         psum = ctx.enter_context(tc.psum_pool(name="psum", bufs=8))
         ctx.enter_context(tc.manual_schedule())
 
-        ident_f = keep.tile([P, P], F32, name="ident_f")
-        make_identity(nc, ident_f[:])
-
         bias_rows = keep.tile([P, CHUNK], BF16, name="bias_rows")
         nc.vector.memset(bias_rows[:], 0.0)
-        ident_b = keep.tile([P, P], BF16, name="ident_b")
-        nc.vector.tensor_copy(out=ident_b[:], in_=ident_f[:])
-
-        planes = []
-        for j, (lo, hi) in enumerate(SCALE_GROUPS):
-            plane = keep.tile([P, PASSES, hi - lo], U8, name="plane%d" % j, align_bytes=64)
-            nc.vector.memset(plane[:].rearrange("p g n -> p (g n)").bitcast(I32), 0)
-            planes.append(plane)
-
+        nc.scalar.dma_start(out=bias_rows[0:BIAS_ROWS, :], in_=bias.rearrange("(j c) -> j c", c=CHUNK))
         x_sb = []
         for m in range(M_TILES):
             xt = keep.tile([P, K], BF16, name="x%d" % m)
             nc.sync.dma_start(out=xt[:], in_=x[m])
             x_sb.append(xt)
 
-        nc.scalar.dma_start(out=bias_rows[0:16, :], in_=bias.rearrange("(j c) -> j c", c=CHUNK))
+        ident_f = keep.tile([P, P], F32, name="ident_f")
+        make_identity(nc, ident_f[:])
+
+        warm = keep.tile([P, CHUNK], BF16, name="warm")
+        nc.vector.memset(warm[:], 0.0)
+        ident_b = keep.tile([P, P], BF16, name="ident_b")
+        nc.vector.tensor_copy(out=ident_b[:], in_=ident_f[:])
+
+        planes = []
+        for j, (lo, hi) in enumerate(SCALE_GROUPS):
+            planes.append(keep.tile([P, PASSES, hi - lo], U8, name="plane%d" % j, align_bytes=64))
+
+        def zero_plane(j):
+            nc.vector.memset(planes[j][:].rearrange("p g n -> p (g n)").bitcast(I32), 0)
+
+        zero_plane(0)
+        zero_plane(1)
+        zero_plane(2)
 
         scale_rows = w_scales.rearrange("g (h q) n -> h q g n", h=2)
         words_by_p = w_words.rearrange("g p b -> p g b")
@@ -97,21 +106,18 @@ def tile_quantizedlinear_kernel(tc, x, w_words, w_scales, bias, out):
                         in_=scale_rows[:, 4 * b + r, :, lo:hi].bitcast(view),
                     )
 
-        words = {}
-
-        def load_words(i):
-            lo, hi = WORD_PIECES[i]
+        load_scales(0, nc.sync, I32)
+        words = []
+        for i, (lo, hi) in enumerate(WORD_PIECES):
             wt = keep.tile([P, PASSES, 2 * (hi - lo)], U8, name="w%d" % i, align_bytes=64)
             nc.sync.dma_start(out=wt[:].bitcast(I32), in_=words_by_p[:, :, 2 * lo : 2 * hi].bitcast(I32))
-            words[i] = wt
+            words.append(wt)
+        load_scales(1, nc.gpsimd, F32)
+        load_scales(2, nc.gpsimd, F32)
 
-        for kind, i in SYNC_LOADS:
-            if kind == "s":
-                load_scales(i, nc.sync, I32)
-            else:
-                load_words(i)
-        for j in GPSIMD_SCALES:
-            load_scales(j, nc.gpsimd, F32)
+        dummy = psum.tile([P, CHUNK], F32, tag="bank", name="dummy")
+        for i in range(N_DUMMIES):
+            nc.tensor.matmul(dummy[:], lhsT=warm[:, 0:P], rhs=warm[:], start=True, stop=True)
 
         bias_bc = keep.tile([P, N], BF16, name="bias_bc")
 
@@ -133,21 +139,20 @@ def tile_quantizedlinear_kernel(tc, x, w_words, w_scales, bias, out):
         xq = keep.tile([P, M_TILES * PASSES * P], U32, name="xq", align_bytes=64)
         xs = keep.tile([P, M_TILES * PASSES * P], U8, name="xs", align_bytes=64)
 
-        def transpose_x(m):
+        def transpose_x(m, half):
             xw = x_sb[m][:].bitcast(F32)
-            for half in range(2):
-                tp = psum.tile([P, 2, 2, P], F32, tag="bank", name="tp")
-                for a in range(2):
-                    g = 2 * half + a
-                    for u in range(2):
-                        nc.tensor.transpose(tp[:, a, u, :], xw[:, 256 * g + u : 256 * (g + 1) : 2], ident_f[:])
-                unit = m * PASSES + 2 * half
-                dst = grouped_w[:, unit * 2 * P : (unit + 2) * 2 * P].rearrange("p (a r u) -> p a r u", a=2, u=2)
-                src = tp[:].rearrange("p a u r -> p a r u")
-                if half == 0:
-                    nc.vector.tensor_copy(out=dst, in_=src)
-                else:
-                    nc.scalar.copy(out=dst, in_=src)
+            tp = psum.tile([P, 2, 2, P], F32, tag="bank", name="tp")
+            for a in range(2):
+                g = 2 * half + a
+                for u in range(2):
+                    nc.tensor.transpose(tp[:, a, u, :], xw[:, 256 * g + u : 256 * (g + 1) : 2], ident_f[:])
+            unit = m * PASSES + 2 * half
+            dst = grouped_w[:, unit * 2 * P : (unit + 2) * 2 * P].rearrange("p (a r u) -> p a r u", a=2, u=2)
+            src = tp[:].rearrange("p a u r -> p a r u")
+            if half == 0:
+                nc.vector.tensor_copy(out=dst, in_=src)
+            else:
+                nc.scalar.copy(out=dst, in_=src)
 
         def quantise_x(m):
             w = PASSES * P
@@ -159,14 +164,18 @@ def tile_quantizedlinear_kernel(tc, x, w_words, w_scales, bias, out):
 
         spread_bias(0)
         spread_bias(1)
-        transpose_x(0)
-        transpose_x(1)
+        transpose_x(0, 0)
+        spread_bias(2)
+        transpose_x(0, 1)
+        transpose_x(1, 0)
+        spread_bias(3)
+        transpose_x(1, 1)
         quantise_x(0)
         quantise_x(1)
-        for t in range(2, N_CHUNKS // 2):
+        for t in range(4, N_CHUNKS // 2):
             spread_bias(t)
 
-        def product(m, lo, width, ot, slo):
+        def product(c, m, lo, width, ot, slo):
             jg, glo = find_piece(SCALE_GROUPS, lo)
             iw, wlo = find_piece(WORD_PIECES, lo)
             acc = psum.tile([P, width], F32, tag="bank", name="acc")
@@ -200,15 +209,19 @@ def tile_quantizedlinear_kernel(tc, x, w_words, w_scales, bias, out):
                 ot = o_tiles[(si, m)]
                 if last and m == M_TILES - 1:
                     for q in range(CHUNK // TAIL_N):
-                        product(m, col + q * TAIL_N, TAIL_N, ot, slo)
+                        product(c, m, col + q * TAIL_N, TAIL_N, ot, slo)
                         if q % 2 == 1:
                             a = col + (q - 1) * TAIL_N
                             b = col + (q + 1) * TAIL_N
-                            nc.scalar.dma_start(out=out[m, :, a:b], in_=ot[:, a - slo : b - slo])
+                            nc.sync.dma_start(out=out[m, :, a:b], in_=ot[:, a - slo : b - slo])
                 else:
-                    product(m, col, CHUNK, ot, slo)
+                    product(c, m, col, CHUNK, ot, slo)
                     if last:
-                        nc.scalar.dma_start(out=out[m, :, slo:shi], in_=ot[:])
+                        nc.sync.dma_start(out=out[m, :, slo:shi], in_=ot[:])
             if col + CHUNK == shi and not last:
                 for m in range(M_TILES):
                     nc.scalar.dma_start(out=out[m, :, slo:shi], in_=o_tiles[(si, m)][:])
+            for j in GPSIMD_SCALES:
+                if ZERO_AFTER_CHUNK.get(j) == c:
+                    zero_plane(j)
+                    load_scales(j, nc.gpsimd, F32)

@@ -112,7 +112,12 @@ def tile_quantizedlinear_kernel(tc, x, w_words, w_scales, bias, out):
             wt = keep.tile([P, PASSES, 2 * (hi - lo)], U8, name="w%d" % i, align_bytes=64)
             nc.sync.dma_start(out=wt[:].bitcast(I32), in_=words_by_p[:, :, 2 * lo : 2 * hi].bitcast(I32))
             words.append(wt)
-        load_scales(1, nc.gpsimd, F32)
+        scale_rows4 = w_scales.rearrange("g (a r) n -> a r g n", r=4)
+        lo1, hi1 = SCALE_GROUPS[1]
+        for r in range(4):
+            nc.gpsimd.dma_start(
+                out=planes[1][r:P:32, :, :].bitcast(F32), in_=scale_rows4[:, r, :, lo1:hi1].bitcast(F32)
+            )
         load_scales(2, nc.gpsimd, F32)
 
         dummy = psum.tile([P, CHUNK], F32, tag="bank", name="dummy")

from contextlib import ExitStack

import concourse.mybir as mybir
from concourse.masks import make_identity

BF16 = mybir.dt.bfloat16
F32 = mybir.dt.float32
I32 = mybir.dt.int32
U8 = mybir.dt.uint8
U32 = mybir.dt.uint32
FP8X4 = mybir.dt.float8_e4m3fn_x4
FP4X4 = mybir.dt.float4_e2m1fn_x4

P = 128
K = 2048
N = 8192
M_TILES = 2
PASSES = K // 512
CHUNK = 512
N_CHUNKS = N // CHUNK
BIAS_ROWS = N // CHUNK

FLOPS = 2 * M_TILES * P * K * N

SCALE_GROUPS = [(0, 2048), (2048, 4096), (4096, 6144), (6144, 8192)]
WORD_PIECES = [
    (0, 512),
    (512, 1024),
    (1024, 2048),
    (2048, 3072),
    (3072, 4096),
    (4096, 5120),
    (5120, 6144),
    (6144, 7168),
    (7168, 7680),
    (7680, 8192),
]
STORE_PIECES = [
    (0, 1024),
    (1024, 2048),
    (2048, 3072),
    (3072, 4096),
    (4096, 5120),
    (5120, 6144),
    (6144, 7168),
    (7168, 7680),
    (7680, 8192),
]
GPSIMD_SCALES = [1, 2, 3]
ZERO_AFTER_CHUNK = {3: 1}
N_DUMMIES = 4
TAIL_N = 128


def find_piece(pieces, col):
    for i, (lo, hi) in enumerate(pieces):
        if lo <= col < hi:
            return i, lo
    raise ValueError("column outside every piece")


def tile_quantizedlinear_kernel(tc, x, w_words, w_scales, bias, out):
    nc = tc.nc
    with ExitStack() as ctx:
        keep = ctx.enter_context(tc.tile_pool(name="keep", bufs=1))
        psum = ctx.enter_context(tc.psum_pool(name="psum", bufs=8))
        ctx.enter_context(tc.manual_schedule())

        bias_rows = keep.tile([P, CHUNK], BF16, name="bias_rows")
        nc.vector.memset(bias_rows[:], 0.0)
        nc.scalar.dma_start(out=bias_rows[0:BIAS_ROWS, :], in_=bias.rearrange("(j c) -> j c", c=CHUNK))
        x_sb = []
        for m in range(M_TILES):
            xt = keep.tile([P, K], BF16, name="x%d" % m)
            nc.sync.dma_start(out=xt[:], in_=x[m])
            x_sb.append(xt)

        ident_f = keep.tile([P, P], F32, name="ident_f")
        make_identity(nc, ident_f[:])

        warm = keep.tile([P, CHUNK], BF16, name="warm")
        nc.vector.memset(warm[:], 0.0)
        ident_b = keep.tile([P, P], BF16, name="ident_b")
        nc.vector.tensor_copy(out=ident_b[:], in_=ident_f[:])

        planes = []
        for j, (lo, hi) in enumerate(SCALE_GROUPS):
            planes.append(keep.tile([P, PASSES, hi - lo], U8, name="plane%d" % j, align_bytes=64))

        def zero_plane(j):
            nc.vector.memset(planes[j][:].rearrange("p g n -> p (g n)").bitcast(I32), 0)

        zero_plane(0)
        zero_plane(1)
        zero_plane(2)

        scale_rows = w_scales.rearrange("g (h q) n -> h q g n", h=2)
        words_by_p = w_words.rearrange("g p b -> p g b")

        def load_scales(j, queue, view):
            lo, hi = SCALE_GROUPS[j]
            for b in range(2):
                for r in range(4):
                    queue.dma_start(
                        out=planes[j][32 * b + r : P : 64, :, :].bitcast(view),
                        in_=scale_rows[:, 4 * b + r, :, lo:hi].bitcast(view),
                    )

        load_scales(0, nc.sync, I32)
        words = []
        for i, (lo, hi) in enumerate(WORD_PIECES):
            wt = keep.tile([P, PASSES, 2 * (hi - lo)], U8, name="w%d" % i, align_bytes=64)
            nc.sync.dma_start(out=wt[:].bitcast(I32), in_=words_by_p[:, :, 2 * lo : 2 * hi].bitcast(I32))
            words.append(wt)
        scale_rows4 = w_scales.rearrange("g (a r) n -> a r g n", r=4)
        lo1, hi1 = SCALE_GROUPS[1]
        for r in range(4):
            nc.gpsimd.dma_start(
                out=planes[1][r:P:32, :, :].bitcast(F32), in_=scale_rows4[:, r, :, lo1:hi1].bitcast(F32)
            )
        load_scales(2, nc.gpsimd, F32)

        dummy = psum.tile([P, CHUNK], F32, tag="bank", name="dummy")
        for i in range(N_DUMMIES):
            nc.tensor.matmul(dummy[:], lhsT=warm[:, 0:P], rhs=warm[:], start=True, stop=True)

        bias_bc = keep.tile([P, N], BF16, name="bias_bc")

        def spread_bias(t):
            bp = psum.tile([P, 2 * CHUNK], BF16, tag="bank", name="bp")
            for h in range(2):
                j = 2 * t + h
                nc.tensor.matmul(
                    bp[:, h * CHUNK : (h + 1) * CHUNK],
                    lhsT=ident_b[:, j : j + 1].to_broadcast([P, P]),
                    rhs=bias_rows[:],
                    start=True,
                    stop=True,
                )
            nc.scalar.copy(out=bias_bc[:, 2 * t * CHUNK : 2 * (t + 1) * CHUNK], in_=bp[:])

        grouped = keep.tile([P, M_TILES * PASSES * P * 4], BF16, name="grouped", align_bytes=64)
        grouped_w = grouped[:].bitcast(F32)
        xq = keep.tile([P, M_TILES * PASSES * P], U32, name="xq", align_bytes=64)
        xs = keep.tile([P, M_TILES * PASSES * P], U8, name="xs", align_bytes=64)

        def transpose_x(m, half):
            xw = x_sb[m][:].bitcast(F32)
            tp = psum.tile([P, 2, 2, P], F32, tag="bank", name="tp")
            for a in range(2):
                g = 2 * half + a
                for u in range(2):
                    nc.tensor.transpose(tp[:, a, u, :], xw[:, 256 * g + u : 256 * (g + 1) : 2], ident_f[:])
            unit = m * PASSES + 2 * half
            dst = grouped_w[:, unit * 2 * P : (unit + 2) * 2 * P].rearrange("p (a r u) -> p a r u", a=2, u=2)
            src = tp[:].rearrange("p a u r -> p a r u")
            if half == 0:
                nc.vector.tensor_copy(out=dst, in_=src)
            else:
                nc.scalar.copy(out=dst, in_=src)

        def quantise_x(m):
            w = PASSES * P
            nc.vector.quantize_mx(
                out=xq[:, m * w : (m + 1) * w].bitcast(FP8X4),
                scales=xs[:, m * w : (m + 1) * w],
                in_=grouped[:, m * 4 * w : (m + 1) * 4 * w],
            )

        spread_bias(0)
        spread_bias(1)
        transpose_x(0, 0)
        spread_bias(2)
        transpose_x(0, 1)
        transpose_x(1, 0)
        spread_bias(3)
        transpose_x(1, 1)
        quantise_x(0)
        quantise_x(1)
        for t in range(4, N_CHUNKS // 2):
            spread_bias(t)

        def product(c, m, lo, width, ot, slo):
            jg, glo = find_piece(SCALE_GROUPS, lo)
            iw, wlo = find_piece(WORD_PIECES, lo)
            acc = psum.tile([P, width], F32, tag="bank", name="acc")
            for g in range(PASSES):
                unit = m * PASSES + g
                nc.tensor.matmul_mx(
                    out=acc[:],
                    lhsT=xq[:, unit * P : (unit + 1) * P].bitcast(FP8X4),
                    lhsT_scale=xs[:, unit * P : (unit + 1) * P],
                    rhs=words[iw][:, g, 2 * (lo - wlo) : 2 * (lo - wlo + width)].bitcast(FP4X4),
                    rhs_scale=planes[jg][:, g, lo - glo : lo - glo + width],
                    start=(g == 0),
                    stop=(g == PASSES - 1),
                )
            nc.vector.tensor_tensor(
                out=ot[:, lo - slo : lo - slo + width],
                in0=acc[:],
                in1=bias_bc[:, lo : lo + width],
                op=mybir.AluOpType.add,
            )

        o_tiles = {}
        for c in range(N_CHUNKS):
            col = c * CHUNK
            si, slo = find_piece(STORE_PIECES, col)
            shi = STORE_PIECES[si][1]
            last = c == N_CHUNKS - 1
            for m in range(M_TILES):
                if (si, m) not in o_tiles:
                    o_tiles[(si, m)] = keep.tile([P, shi - slo], F32, name="o%d_%d" % (si, m))
                ot = o_tiles[(si, m)]
                if last and m == M_TILES - 1:
                    for q in range(CHUNK // TAIL_N):
                        product(c, m, col + q * TAIL_N, TAIL_N, ot, slo)
                        if q % 2 == 1:
                            a = col + (q - 1) * TAIL_N
                            b = col + (q + 1) * TAIL_N
                            nc.sync.dma_start(out=out[m, :, a:b], in_=ot[:, a - slo : b - slo])
                else:
                    product(c, m, col, CHUNK, ot, slo)
                    if last:
                        nc.sync.dma_start(out=out[m, :, slo:shi], in_=ot[:])
            if col + CHUNK == shi and not last:
                for m in range(M_TILES):
                    nc.scalar.dma_start(out=out[m, :, slo:shi], in_=o_tiles[(si, m)][:])
            for j in GPSIMD_SCALES:
                if ZERO_AFTER_CHUNK.get(j) == c:
                    zero_plane(j)
                    load_scales(j, nc.gpsimd, F32)
